import numpy as np
import ml_dtypes

BF16 = ml_dtypes.bfloat16


def bf(x):
    return np.asarray(x, np.float32).astype(BF16)


def f32(x):
    return np.asarray(x, np.float32)


def f64(x):
    return np.asarray(x).astype(np.float64)


def striped(idx):
    return np.tile(idx.reshape(-1, 16).T, (8, 1))


C, S, K, H, N = 768, 256, 4, 128, 512


def setup_inputs():
    idx = np.concatenate([np.random.permutation(S)[:H] for _ in range(K)])
    return {"feat": f32(np.random.standard_normal((C, S))), "code_w": f32(0.1 * np.random.standard_normal((C, N))), "code_bias": f32(0.5 * np.random.standard_normal((1, N))), "offs": striped(idx)}


def reference(feat, code_w, code_bias, offs):
    idx = offs[:16].T.reshape(-1)
    prod = f64(feat)[:, idx] * f64(code_w)
    return prod.sum(axis=0, keepdims=True) + f64(code_bias)

@@ -1,0 +1,63 @@
+import concourse.mybir as mybir
+
+F32 = mybir.dt.float32
+U16 = mybir.dt.uint16
+MULT = mybir.AluOpType.mult
+ADD = mybir.AluOpType.add
+
+P = 128
+C = 768
+S = 256
+N = 512
+BLOCKS = C // P
+HALF = S
+HALVES = N // HALF
+HALF_OFFS = HALF // 16
+
+FLOPS = 2 * C * N
+
+
+def tile_sequentialtask_kernel(tc, feat, code_w, code_bias, offs, out):
+    nc = tc.nc
+    feat_blocks = feat.rearrange("(b p) s -> b p s", p=P)
+    code_w_blocks = code_w.rearrange("(b p) n -> b p n", p=P)
+
+    with (
+        tc.tile_pool(name="held", bufs=1) as held,
+        tc.tile_pool(name="products", bufs=4) as products,
+        tc.psum_pool(name="sums", bufs=1) as sums,
+    ):
+        offsets = held.tile([P, N // 16], U16, name="offsets")
+        nc.sync.dma_start(offsets[:], offs)
+        windows = []
+        weights = []
+        for b in range(BLOCKS):
+            window = held.tile([P, S], F32, name=f"window{b}")
+            nc.sync.dma_start(window[:], feat_blocks[b])
+            windows.append(window)
+            weight = held.tile([P, N], F32, name=f"weight{b}")
+            nc.sync.dma_start(weight[:], code_w_blocks[b])
+            weights.append(weight)
+        bias = held.tile([1, N], F32, name="bias")
+        nc.scalar.dma_start(bias[:], code_bias)
+
+        ones = held.tile([P, 1], F32, name="ones")
+        nc.vector.memset(ones[:], 1.0)
+
+        logit_sums = [sums.tile([1, HALF], F32, name=f"logit_sum{h}") for h in range(HALVES)]
+
+        for b in range(BLOCKS):
+            for h in range(HALVES):
+                columns = slice(h * HALF, (h + 1) * HALF)
+                picked = windows[b][:].indirect(offsets[:, h * HALF_OFFS : (h + 1) * HALF_OFFS])
+                product = products.tile([P, HALF], F32, name="product")
+                nc.vector.tensor_tensor(product[:], picked, weights[b][:, columns], MULT)
+                nc.tensor.matmul(
+                    logit_sums[h][:], ones[:], product[:], start=(b == 0), stop=(b == BLOCKS - 1)
+                )
+
+        logits = held.tile([1, N], F32, name="logits")
+        for h in range(HALVES):
+            columns = slice(h * HALF, (h + 1) * HALF)
+            nc.vector.tensor_tensor(logits[:, columns], logit_sums[h][:], bias[:, columns], ADD)
+        nc.sync.dma_start(out, logits[:])

@@ -35,11 +35,12 @@ def tile_sequentialtask_kernel(tc, feat, code_w, code_bias, offs, out):
             window = held.tile([P, S], F32, name=f"window{b}")
             nc.sync.dma_start(window[:], feat_blocks[b])
             windows.append(window)
-            weight = held.tile([P, N], F32, name=f"weight{b}")
-            nc.sync.dma_start(weight[:], code_w_blocks[b])
-            weights.append(weight)
+            for h in range(HALVES):
+                weight = held.tile([P, HALF], F32, name=f"weight{b}_{h}")
+                nc.scalar.dma_start(weight[:], code_w_blocks[b][:, h * HALF : (h + 1) * HALF])
+                weights.append(weight)
         bias = held.tile([1, N], F32, name="bias")
-        nc.scalar.dma_start(bias[:], code_bias)
+        nc.sync.dma_start(bias[:], code_bias)
 
         ones = held.tile([P, 1], F32, name="ones")
         nc.vector.memset(ones[:], 1.0)
@@ -48,10 +49,9 @@ def tile_sequentialtask_kernel(tc, feat, code_w, code_bias, offs, out):
 
         for b in range(BLOCKS):
             for h in range(HALVES):
-                columns = slice(h * HALF, (h + 1) * HALF)
                 picked = windows[b][:].indirect(offsets[:, h * HALF_OFFS : (h + 1) * HALF_OFFS])
                 product = products.tile([P, HALF], F32, name="product")
-                nc.vector.tensor_tensor(product[:], picked, weights[b][:, columns], MULT)
+                nc.vector.tensor_tensor(product[:], picked, weights[b * HALVES + h][:], MULT)
                 nc.tensor.matmul(
                     logit_sums[h][:], ones[:], product[:], start=(b == 0), stop=(b == BLOCKS - 1)
                 )

@@ -13,6 +13,7 @@ BLOCKS = C // P
 HALF = S
 HALVES = N // HALF
 HALF_OFFS = HALF // 16
+WARM_UPS = 4
 
 FLOPS = 2 * C * N
 
@@ -44,6 +45,12 @@ def tile_sequentialtask_kernel(tc, feat, code_w, code_bias, offs, out):
 
         ones = held.tile([P, 1], F32, name="ones")
         nc.vector.memset(ones[:], 1.0)
+
+        zeros = held.tile([P, HALF], F32, name="zeros")
+        nc.vector.memset(zeros[:], 0.0)
+        unread_sum = sums.tile([1, HALF], F32, name="unread_sum")
+        for w in range(WARM_UPS):
+            nc.tensor.matmul(unread_sum[:], ones[:], zeros[:], start=True, stop=True)
 
         logit_sums = [sums.tile([1, HALF], F32, name=f"logit_sum{h}") for h in range(HALVES)]
 

@@ -13,7 +13,9 @@ BLOCKS = C // P
 HALF = S
 HALVES = N // HALF
 HALF_OFFS = HALF // 16
-WARM_UPS = 4
+STRIP = 32
+QUARTERS = P // STRIP
+QUARTER = N // QUARTERS
 
 FLOPS = 2 * C * N
 
@@ -40,31 +42,35 @@ def tile_sequentialtask_kernel(tc, feat, code_w, code_bias, offs, out):
                 weight = held.tile([P, HALF], F32, name=f"weight{b}_{h}")
                 nc.scalar.dma_start(weight[:], code_w_blocks[b][:, h * HALF : (h + 1) * HALF])
                 weights.append(weight)
-        bias = held.tile([1, N], F32, name="bias")
-        nc.sync.dma_start(bias[:], code_bias)
 
-        ones = held.tile([P, 1], F32, name="ones")
+        bias = held.tile([P, QUARTER], F32, name="bias")
+        for q in range(QUARTERS):
+            nc.gpsimd.dma_start(
+                bias[q * STRIP : (q + 1) * STRIP, :],
+                code_bias[:, q * QUARTER : (q + 1) * QUARTER].to_broadcast([STRIP, QUARTER]),
+            )
+
+        ones = held.tile([P, STRIP], F32, name="ones")
         nc.vector.memset(ones[:], 1.0)
-
-        zeros = held.tile([P, HALF], F32, name="zeros")
-        nc.vector.memset(zeros[:], 0.0)
-        unread_sum = sums.tile([1, HALF], F32, name="unread_sum")
-        for w in range(WARM_UPS):
-            nc.tensor.matmul(unread_sum[:], ones[:], zeros[:], start=True, stop=True)
-
-        logit_sums = [sums.tile([1, HALF], F32, name=f"logit_sum{h}") for h in range(HALVES)]
+        logit_sums = sums.tile([P, QUARTER], F32, name="logit_sums")
 
         for b in range(BLOCKS):
             for h in range(HALVES):
                 picked = windows[b][:].indirect(offsets[:, h * HALF_OFFS : (h + 1) * HALF_OFFS])
                 product = products.tile([P, HALF], F32, name="product")
                 nc.vector.tensor_tensor(product[:], picked, weights[b * HALVES + h][:], MULT)
-                nc.tensor.matmul(
-                    logit_sums[h][:], ones[:], product[:], start=(b == 0), stop=(b == BLOCKS - 1)
-                )
+                for k in range(HALF // QUARTER):
+                    q = h * (HALF // QUARTER) + k
+                    nc.tensor.matmul(
+                        logit_sums[q * STRIP : (q + 1) * STRIP, :],
+                        ones[:],
+                        product[:, k * QUARTER : (k + 1) * QUARTER],
+                        start=(b == 0),
+                        stop=(b == BLOCKS - 1),
+                    )
 
-        logits = held.tile([1, N], F32, name="logits")
-        for h in range(HALVES):
-            columns = slice(h * HALF, (h + 1) * HALF)
-            nc.vector.tensor_tensor(logits[:, columns], logit_sums[h][:], bias[:, columns], ADD)
-        nc.sync.dma_start(out, logits[:])
+        logits = held.tile([P, QUARTER], F32, name="logits")
+        nc.vector.tensor_tensor(logits[:], logit_sums[:], bias[:], ADD)
+        for q in range(QUARTERS):
+            queue = nc.sync if q % 2 == 0 else nc.scalar
+            queue.dma_start(out[:, q * QUARTER : (q + 1) * QUARTER], logits[q * STRIP : q * STRIP + 1, :])

@@ -45,7 +45,7 @@ def tile_sequentialtask_kernel(tc, feat, code_w, code_bias, offs, out):
 
         bias = held.tile([P, QUARTER], F32, name="bias")
         for q in range(QUARTERS):
-            nc.gpsimd.dma_start(
+            nc.sync.dma_start(
                 bias[q * STRIP : (q + 1) * STRIP, :],
                 code_bias[:, q * QUARTER : (q + 1) * QUARTER].to_broadcast([STRIP, QUARTER]),
             )
@@ -71,6 +71,4 @@ def tile_sequentialtask_kernel(tc, feat, code_w, code_bias, offs, out):
 
         logits = held.tile([P, QUARTER], F32, name="logits")
         nc.vector.tensor_tensor(logits[:], logit_sums[:], bias[:], ADD)
-        for q in range(QUARTERS):
-            queue = nc.sync if q % 2 == 0 else nc.scalar
-            queue.dma_start(out[:, q * QUARTER : (q + 1) * QUARTER], logits[q * STRIP : q * STRIP + 1, :])
+        nc.sync.dma_start(out.rearrange("o (q n) -> (o q) n", q=QUARTERS), logits[0:P:STRIP, :])

@@ -14,8 +14,8 @@ HALF = S
 HALVES = N // HALF
 HALF_OFFS = HALF // 16
 STRIP = 32
-QUARTERS = P // STRIP
-QUARTER = N // QUARTERS
+STRIPS = P // STRIP
+SHARE = HALF // STRIPS
 
 FLOPS = 2 * C * N
 
@@ -43,32 +43,35 @@ def tile_sequentialtask_kernel(tc, feat, code_w, code_bias, offs, out):
                 nc.scalar.dma_start(weight[:], code_w_blocks[b][:, h * HALF : (h + 1) * HALF])
                 weights.append(weight)
 
-        bias = held.tile([P, QUARTER], F32, name="bias")
-        for q in range(QUARTERS):
+        bias = held.tile([P, HALVES, SHARE], F32, name="bias")
+        bias_shares = code_bias.rearrange("o (h q i) -> q o h i", h=HALVES, q=STRIPS)
+        for q in range(STRIPS):
             nc.sync.dma_start(
-                bias[q * STRIP : (q + 1) * STRIP, :],
-                code_bias[:, q * QUARTER : (q + 1) * QUARTER].to_broadcast([STRIP, QUARTER]),
+                bias[q * STRIP : (q + 1) * STRIP, :, :],
+                bias_shares[q].to_broadcast([STRIP, HALVES, SHARE]),
             )
 
         ones = held.tile([P, STRIP], F32, name="ones")
         nc.vector.memset(ones[:], 1.0)
-        logit_sums = sums.tile([P, QUARTER], F32, name="logit_sums")
+        logit_sums = [sums.tile([P, SHARE], F32, name=f"logit_sums{h}") for h in range(HALVES)]
 
         for b in range(BLOCKS):
             for h in range(HALVES):
                 picked = windows[b][:].indirect(offsets[:, h * HALF_OFFS : (h + 1) * HALF_OFFS])
                 product = products.tile([P, HALF], F32, name="product")
                 nc.vector.tensor_tensor(product[:], picked, weights[b * HALVES + h][:], MULT)
-                for k in range(HALF // QUARTER):
-                    q = h * (HALF // QUARTER) + k
+                for q in range(STRIPS):
                     nc.tensor.matmul(
-                        logit_sums[q * STRIP : (q + 1) * STRIP, :],
+                        logit_sums[h][q * STRIP : (q + 1) * STRIP, :],
                         ones[:],
-                        product[:, k * QUARTER : (k + 1) * QUARTER],
+                        product[:, q * SHARE : (q + 1) * SHARE],
                         start=(b == 0),
                         stop=(b == BLOCKS - 1),
                     )
 
-        logits = held.tile([P, QUARTER], F32, name="logits")
-        nc.vector.tensor_tensor(logits[:], logit_sums[:], bias[:], ADD)
-        nc.sync.dma_start(out.rearrange("o (q n) -> (o q) n", q=QUARTERS), logits[0:P:STRIP, :])
+        logits = held.tile([P, HALVES, SHARE], F32, name="logits")
+        for h in range(HALVES):
+            nc.vector.tensor_tensor(logits[:, h, :], logit_sums[h][:], bias[:, h, :], ADD)
+        nc.sync.dma_start(
+            out.rearrange("o (h q i) -> (o q) h i", h=HALVES, q=STRIPS), logits[0:P:STRIP, :, :]
+        )

@@ -46,7 +46,7 @@ def tile_sequentialtask_kernel(tc, feat, code_w, code_bias, offs, out):
         bias = held.tile([P, HALVES, SHARE], F32, name="bias")
         bias_shares = code_bias.rearrange("o (h q i) -> q o h i", h=HALVES, q=STRIPS)
         for q in range(STRIPS):
-            nc.sync.dma_start(
+            nc.scalar.dma_start(
                 bias[q * STRIP : (q + 1) * STRIP, :, :],
                 bias_shares[q].to_broadcast([STRIP, HALVES, SHARE]),
             )

@@ -38,18 +38,19 @@ def tile_sequentialtask_kernel(tc, feat, code_w, code_bias, offs, out):
             window = held.tile([P, S], F32, name=f"window{b}")
             nc.sync.dma_start(window[:], feat_blocks[b])
             windows.append(window)
-            for h in range(HALVES):
-                weight = held.tile([P, HALF], F32, name=f"weight{b}_{h}")
-                nc.scalar.dma_start(weight[:], code_w_blocks[b][:, h * HALF : (h + 1) * HALF])
-                weights.append(weight)
+            loads = HALVES if b == 0 else 1
+            width = N // loads
+            for k in range(loads):
+                weight = held.tile([P, width], F32, name=f"weight{b}_{k}")
+                nc.scalar.dma_start(weight[:], code_w_blocks[b][:, k * width : (k + 1) * width])
+                for start in range(0, width, HALF):
+                    weights.append(weight[:, start : start + HALF])
 
         bias = held.tile([P, HALVES, SHARE], F32, name="bias")
-        bias_shares = code_bias.rearrange("o (h q i) -> q o h i", h=HALVES, q=STRIPS)
-        for q in range(STRIPS):
-            nc.scalar.dma_start(
-                bias[q * STRIP : (q + 1) * STRIP, :, :],
-                bias_shares[q].to_broadcast([STRIP, HALVES, SHARE]),
-            )
+        nc.vector.memset(bias[:], 0.0)
+        nc.scalar.dma_start(
+            bias[0:P:STRIP, :, :], code_bias.rearrange("o (h q i) -> (o q) h i", h=HALVES, q=STRIPS)
+        )
 
         ones = held.tile([P, STRIP], F32, name="ones")
         nc.vector.memset(ones[:], 1.0)
@@ -59,7 +60,7 @@ def tile_sequentialtask_kernel(tc, feat, code_w, code_bias, offs, out):
             for h in range(HALVES):
                 picked = windows[b][:].indirect(offsets[:, h * HALF_OFFS : (h + 1) * HALF_OFFS])
                 product = products.tile([P, HALF], F32, name="product")
-                nc.vector.tensor_tensor(product[:], picked, weights[b * HALVES + h][:], MULT)
+                nc.vector.tensor_tensor(product[:], picked, weights[b * HALVES + h], MULT)
                 for q in range(STRIPS):
                     nc.tensor.matmul(
                         logit_sums[h][q * STRIP : (q + 1) * STRIP, :],

@@ -54,25 +54,29 @@ def tile_sequentialtask_kernel(tc, feat, code_w, code_bias, offs, out):
 
         ones = held.tile([P, STRIP], F32, name="ones")
         nc.vector.memset(ones[:], 1.0)
-        logit_sums = [sums.tile([P, SHARE], F32, name=f"logit_sums{h}") for h in range(HALVES)]
+        logit_sums = sums.tile([P, HALVES, SHARE], F32, name="logit_sums")
 
         for b in range(BLOCKS):
+            product = products.tile([P, HALVES, STRIPS, SHARE], F32, name="product")
+            last = b == BLOCKS - 1
             for h in range(HALVES):
                 picked = windows[b][:].indirect(offsets[:, h * HALF_OFFS : (h + 1) * HALF_OFFS])
-                product = products.tile([P, HALF], F32, name="product")
-                nc.vector.tensor_tensor(product[:], picked, weights[b * HALVES + h], MULT)
-                for q in range(STRIPS):
-                    nc.tensor.matmul(
-                        logit_sums[h][q * STRIP : (q + 1) * STRIP, :],
-                        ones[:],
-                        product[:, q * SHARE : (q + 1) * SHARE],
-                        start=(b == 0),
-                        stop=(b == BLOCKS - 1),
-                    )
+                nc.vector.tensor_tensor(
+                    product[:, h].rearrange("p q i -> p (q i)"), picked, weights[b * HALVES + h], MULT
+                )
+                if h == HALVES - 1 or last:
+                    halves = slice(h, h + 1) if last else slice(0, HALVES)
+                    for q in range(STRIPS):
+                        nc.tensor.matmul(
+                            logit_sums[q * STRIP : (q + 1) * STRIP, halves, :],
+                            ones[:],
+                            product[:, halves, q, :],
+                            start=(b == 0),
+                            stop=(last and h == HALVES - 1),
+                        )
 
         logits = held.tile([P, HALVES, SHARE], F32, name="logits")
-        for h in range(HALVES):
-            nc.vector.tensor_tensor(logits[:, h, :], logit_sums[h][:], bias[:, h, :], ADD)
+        nc.vector.tensor_tensor(logits[:], logit_sums[:], bias[:], ADD)
         nc.sync.dma_start(
             out.rearrange("o (h q i) -> (o q) h i", h=HALVES, q=STRIPS), logits[0:P:STRIP, :, :]
         )

import concourse.mybir as mybir

F32 = mybir.dt.float32
U16 = mybir.dt.uint16
MULT = mybir.AluOpType.mult
ADD = mybir.AluOpType.add

P = 128
C = 768
S = 256
N = 512
BLOCKS = C // P
HALF = S
HALVES = N // HALF
HALF_OFFS = HALF // 16
STRIP = 32
STRIPS = P // STRIP
SHARE = HALF // STRIPS

FLOPS = 2 * C * N


def tile_sequentialtask_kernel(tc, feat, code_w, code_bias, offs, out):
    nc = tc.nc
    feat_blocks = feat.rearrange("(b p) s -> b p s", p=P)
    code_w_blocks = code_w.rearrange("(b p) n -> b p n", p=P)

    with (
        tc.tile_pool(name="held", bufs=1) as held,
        tc.tile_pool(name="products", bufs=4) as products,
        tc.psum_pool(name="sums", bufs=1) as sums,
    ):
        offsets = held.tile([P, N // 16], U16, name="offsets")
        nc.sync.dma_start(offsets[:], offs)
        windows = []
        weights = []
        for b in range(BLOCKS):
            window = held.tile([P, S], F32, name=f"window{b}")
            nc.sync.dma_start(window[:], feat_blocks[b])
            windows.append(window)
            loads = HALVES if b == 0 else 1
            width = N // loads
            for k in range(loads):
                weight = held.tile([P, width], F32, name=f"weight{b}_{k}")
                nc.scalar.dma_start(weight[:], code_w_blocks[b][:, k * width : (k + 1) * width])
                for start in range(0, width, HALF):
                    weights.append(weight[:, start : start + HALF])

        bias = held.tile([P, HALVES, SHARE], F32, name="bias")
        nc.vector.memset(bias[:], 0.0)
        nc.scalar.dma_start(
            bias[0:P:STRIP, :, :], code_bias.rearrange("o (h q i) -> (o q) h i", h=HALVES, q=STRIPS)
        )

        ones = held.tile([P, STRIP], F32, name="ones")
        nc.vector.memset(ones[:], 1.0)
        logit_sums = sums.tile([P, HALVES, SHARE], F32, name="logit_sums")

        for b in range(BLOCKS):
            product = products.tile([P, HALVES, STRIPS, SHARE], F32, name="product")
            last = b == BLOCKS - 1
            for h in range(HALVES):
                picked = windows[b][:].indirect(offsets[:, h * HALF_OFFS : (h + 1) * HALF_OFFS])
                nc.vector.tensor_tensor(
                    product[:, h].rearrange("p q i -> p (q i)"), picked, weights[b * HALVES + h], MULT
                )
                if h == HALVES - 1 or last:
                    halves = slice(h, h + 1) if last else slice(0, HALVES)
                    for q in range(STRIPS):
                        nc.tensor.matmul(
                            logit_sums[q * STRIP : (q + 1) * STRIP, halves, :],
                            ones[:],
                            product[:, halves, q, :],
                            start=(b == 0),
                            stop=(last and h == HALVES - 1),
                        )

        logits = held.tile([P, HALVES, SHARE], F32, name="logits")
        nc.vector.tensor_tensor(logits[:], logit_sums[:], bias[:], ADD)
        nc.sync.dma_start(
            out.rearrange("o (h q i) -> (o q) h i", h=HALVES, q=STRIPS), logits[0:P:STRIP, :, :]
        )
